import numpy as np
import ml_dtypes


def mxq(x, axis, fmt="e4m3"):
    dtype, down = {"e4m3": (ml_dtypes.float8_e4m3fn, 7), "e5m2": (ml_dtypes.float8_e5m2, 14)}[fmt]
    v = np.moveaxis(np.asarray(x, np.float32).astype(ml_dtypes.bfloat16).astype(np.float64), axis, -1)
    blocks = v.reshape(v.shape[:-1] + (-1, 32))
    amax = np.abs(blocks).max(-1, keepdims=True)
    byte = np.maximum(np.where(amax > 0, np.frexp(amax)[1] - 1 + 127, 0) - down, 1)
    scale = np.exp2(byte - 127.0)
    codes = (blocks / scale).astype(np.float32).astype(dtype).astype(np.float64)
    return np.moveaxis((codes * scale).reshape(v.shape), -1, axis)


WIDE = False


def mx_kscale(k):
    if not WIDE:
        return np.ones(k)
    levels = np.array([10, -10, 5, -5, 0])
    a = np.random.permutation(np.resize(levels, k // 512 * 4)).reshape(k // 512, 4)
    idx = np.arange(k)
    return np.exp2(a[idx // 512, idx % 128 // 32])


BF16 = ml_dtypes.bfloat16


def bf(x):
    return np.asarray(x, np.float32).astype(BF16)


def f64(x):
    return np.asarray(x).astype(np.float64)


B, S, C, H, D = 8, 1024, 256, 4, 128
E = H * D
EPS = 1e-15


def setup_inputs():
    t = mx_kscale(E)
    return {"q_feat": bf(np.maximum(np.random.standard_normal((B, H, S, D)), 0.0)),
            "vk": bf(np.random.standard_normal((B, H, D, D)) * np.sqrt(S) * t.reshape(H, D)[None, :, :, None]),
            "k_sum": bf(S * (0.11 + 0.02 * np.random.standard_normal((B, H, D)))),
            "Wo": bf(np.random.standard_normal((C, E)) * 6.0 / np.sqrt(E) / t[None, :]),
            "bo": bf(np.random.standard_normal(C) * 0.1)}


def reference(q_feat, vk, k_sum, Wo, bo):
    hs = f64(vk) @ f64(q_feat).transpose(0, 1, 3, 2)
    den = (f64(q_feat) * f64(k_sum)[:, :, None, :]).sum(-1)
    hs = hs / (den[:, :, None, :] + EPS)
    a = hs.transpose(0, 3, 1, 2).reshape(B, S, E)
    return (mxq(a, 2, "e4m3") @ mxq(f64(Wo), 1, "e4m3").T) + f64(bo)

@@ -1,0 +1,206 @@
+from contextlib import ExitStack
+
+import concourse.masks as masks
+import concourse.mybir as mybir
+
+BF16 = mybir.dt.bfloat16
+F32 = mybir.dt.float32
+U32 = mybir.dt.uint32
+U8 = mybir.dt.uint8
+FP8X4 = mybir.dt.float8_e4m3fn_x4
+MULT = mybir.AluOpType.mult
+ADD = mybir.AluOpType.add
+
+B, H, S, D, C = 8, 4, 1024, 128, 256
+E = H * D
+EPS = 1e-15
+
+P = 128
+PACK = 4
+TILES = S // P
+PAIR = 2
+PAIRS = TILES // PAIR
+STEPS = B * PAIRS
+BANK_BLOCKS = 8
+C_TILES = C // P
+
+assert E == P * PACK
+assert H == PACK
+assert H == PAIRS
+
+FLOPS = 2 * B * S * E * C + 2 * B * H * S * D * D + 2 * B * H * S * D
+
+
+def tile_lineartransformerblock_pc_t_kernel(tc, q_feat, vk, k_sum, Wo, bo, out):
+    nc = tc.nc
+    with ExitStack() as ctx:
+        const = ctx.enter_context(tc.tile_pool(name="const", bufs=1))
+        loads = ctx.enter_context(tc.tile_pool(name="loads", bufs=1))
+        per_batch = ctx.enter_context(tc.tile_pool(name="per_batch", bufs=2))
+        per_pair = ctx.enter_context(tc.tile_pool(name="per_pair", bufs=3))
+        psum = ctx.enter_context(tc.psum_pool(name="psum", bufs=1))
+        ctx.enter_context(tc.manual_schedule())
+
+        ident = const.tile([P, P], BF16)
+        masks.make_identity(nc, ident[:])
+
+        ks_rows = const.tile([P, D], BF16)
+        nc.vector.memset(ks_rows[:], 0.0)
+        nc.sync.dma_start(out=ks_rows[0 : B * H, :], in_=k_sum.rearrange("b h d -> (b h) d"))
+
+        vk_sb = {}
+        q_sb = {}
+
+        def load_batch(b):
+            vk_sb[b] = loads.tile([P, H, D], BF16, name="vk_sb%d" % b)
+            nc.sync.dma_start(out=vk_sb[b][:], in_=vk[b].rearrange("h n d -> n h d"))
+            for h in range(H):
+                q_sb[(b, h)] = loads.tile([P, TILES, D], BF16, name="q_sb%d_%d" % (b, h))
+                nc.sync.dma_start(
+                    out=q_sb[(b, h)][:], in_=q_feat[b, h].rearrange("(p i) d -> p i d", i=TILES)
+                )
+
+        load_batch(0)
+        wo_sb = const.tile([P, C_TILES, E], BF16)
+        nc.sync.dma_start(out=wo_sb[:], in_=Wo.rearrange("(k p) e -> p k e", p=P))
+        load_batch(1)
+        bias = const.tile([P, C], BF16)
+        nc.sync.dma_start(out=bias[:], in_=bo.partition_broadcast(P))
+        for b in range(2, B):
+            load_batch(b)
+
+        vkT = {}
+        qT = {}
+        rden = {}
+        a_sb = {}
+        grouped = {}
+        codes = {}
+        scales = {}
+        o_ps = {}
+
+        def transpose_blocks(blocks):
+            bank = psum.tile([P, BANK_BLOCKS, P], BF16, tag="flipped", bufs=4)
+            for j, block in enumerate(blocks):
+                nc.tensor.transpose(bank[:, j, :], block, ident[:])
+            return bank
+
+        def flip_vk(b):
+            bank = transpose_blocks([vk_sb[b][:, h, :] for h in range(H)])
+            vkT[b] = per_batch.tile([P, H, D], BF16, name="vkT", tag="vkT")
+            nc.scalar.copy(out=vkT[b][:], in_=bank[:, 0:H, :])
+
+        def flip_q(b, h):
+            if h == 0:
+                qT[b] = per_batch.tile([P, H, TILES, P], BF16, name="qT", tag="qT")
+            bank = transpose_blocks([q_sb[(b, h)][:, i, :] for i in range(TILES)])
+            nc.scalar.copy(out=qT[b][:, h, :, :], in_=bank[:])
+
+        def denominators(b):
+            den_ps = psum.tile([P, TILES, H], F32, tag="den_ps")
+            for i in range(TILES):
+                for h in range(H):
+                    nc.tensor.matmul(
+                        den_ps[:, i, h : h + 1],
+                        lhsT=qT[b][:, h, i, :],
+                        rhs=ksT[:, b * H + h : b * H + h + 1],
+                        start=True,
+                        stop=True,
+                    )
+            den_sb = per_batch.tile([P, TILES, H], F32, tag="den_sb")
+            nc.vector.tensor_scalar_add(out=den_sb[:], in0=den_ps[:], scalar1=EPS)
+            rden[b] = per_batch.tile([P, TILES, H], F32, name="rden", tag="rden")
+            nc.vector.reciprocal(out=rden[b][:], in_=den_sb[:])
+
+        def read_out(n):
+            b, r = divmod(n, PAIRS)
+            a_sb[n] = per_pair.tile([P, PAIR, H, D], BF16, name="a_sb", tag="a_sb")
+            for j in range(PAIR):
+                i = r * PAIR + j
+                hs_ps = psum.tile([P, H, D], F32, tag="hs_ps", bufs=2)
+                for h in range(H):
+                    nc.tensor.matmul(
+                        hs_ps[:, h, :], lhsT=qT[b][:, h, i, :], rhs=vkT[b][:, h, :], start=True, stop=True
+                    )
+                nc.vector.tensor_tensor(
+                    out=a_sb[n][:, j, :, :],
+                    in0=hs_ps[:],
+                    in1=rden[b][:, i, :].unsqueeze(2).to_broadcast([P, H, D]),
+                    op=MULT,
+                )
+
+        def flip_a(n):
+            bank = transpose_blocks([a_sb[n][:, j, t, :] for j in range(PAIR) for t in range(PACK)])
+            grouped[n] = per_pair.tile([P, PAIR, P, PACK], BF16, name="grouped", tag="grouped", align_bytes=64)
+            nc.scalar.copy(out=grouped[n][:], in_=bank[:].rearrange("p (j t) s -> p j s t", t=PACK))
+
+        def quantise(n):
+            codes[n] = per_pair.tile([P, PAIR * P], U32, name="codes", tag="codes", align_bytes=64)
+            scales[n] = per_pair.tile([P, PAIR * P], U8, name="scales", tag="scales", align_bytes=64)
+            nc.vector.quantize_mx(
+                out=codes[n][:].bitcast(FP8X4),
+                scales=scales[n][:],
+                in_=grouped[n][:].rearrange("p j s t -> p (j s t)"),
+            )
+
+        def project(n):
+            o_ps[n] = psum.tile([P, PAIR, C], F32, name="o_ps", tag="o_ps")
+            for j in range(PAIR):
+                tokens = slice(j * P, (j + 1) * P)
+                nc.tensor.matmul_mx(
+                    out=o_ps[n][:, j, :],
+                    lhsT=codes[n][:, tokens].bitcast(FP8X4),
+                    lhsT_scale=scales[n][:, tokens],
+                    rhs=wo_codes[:].bitcast(FP8X4),
+                    rhs_scale=wo_scales[:],
+                    start=True,
+                    stop=True,
+                )
+
+        def finish(n):
+            b, r = divmod(n, PAIRS)
+            o_sb = per_pair.tile([P, PAIR, C], F32, tag="o_sb", bufs=4)
+            nc.vector.tensor_tensor(
+                out=o_sb[:], in0=o_ps[n][:], in1=bias[:].unsqueeze(1).to_broadcast([P, PAIR, C]), op=ADD
+            )
+            rows = out[b].rearrange("(p i) c -> p i c", i=TILES)
+            nc.sync.dma_start(out=rows[:, r * PAIR : (r + 1) * PAIR, :], in_=o_sb[:])
+
+        bank = transpose_blocks([ks_rows[:]])
+        ksT = const.tile([P, B * H], BF16)
+        nc.scalar.copy(out=ksT[:], in_=bank[:, 0, 0 : B * H])
+
+        flip_vk(0)
+        for h in range(H):
+            flip_q(0, h)
+        denominators(0)
+
+        bank = transpose_blocks(
+            [wo_sb[:, k, t * P : (t + 1) * P] for t in range(PACK) for k in range(C_TILES)]
+        )
+        wo_grouped = const.tile([P, C, PACK], BF16, align_bytes=64)
+        nc.scalar.copy(out=wo_grouped[:], in_=bank[:].rearrange("p (t k) c -> p (k c) t", t=PACK))
+        wo_codes = const.tile([P, C], U32, align_bytes=64)
+        wo_scales = const.tile([P, C], U8, align_bytes=64)
+        nc.vector.quantize_mx(
+            out=wo_codes[:].bitcast(FP8X4), scales=wo_scales[:], in_=wo_grouped[:].rearrange("p c t -> p (c t)")
+        )
+
+        for n in range(STEPS + 3):
+            b, r = divmod(n, PAIRS)
+            next_batch = n < STEPS and b + 1 < B
+            if n >= 3:
+                finish(n - 3)
+            if 2 <= n < STEPS + 2:
+                quantise(n - 2)
+            if next_batch and r == 0:
+                flip_vk(b + 1)
+            if next_batch:
+                flip_q(b + 1, r)
+            if 1 <= n < STEPS + 1:
+                flip_a(n - 1)
+            if n < STEPS:
+                read_out(n)
+            if 2 <= n < STEPS + 2:
+                project(n - 2)
+            if next_batch and r == PAIRS - 1:
+                denominators(b + 1)

@@ -8,8 +8,8 @@ F32 = mybir.dt.float32
 U32 = mybir.dt.uint32
 U8 = mybir.dt.uint8
 FP8X4 = mybir.dt.float8_e4m3fn_x4
-MULT = mybir.AluOpType.mult
 ADD = mybir.AluOpType.add
+COPY = mybir.ActivationFunctionType.Copy
 
 B, H, S, D, C = 8, 4, 1024, 128, 256
 E = H * D
@@ -60,9 +60,9 @@ def tile_lineartransformerblock_pc_t_kernel(tc, q_feat, vk, k_sum, Wo, bo, out):
                     out=q_sb[(b, h)][:], in_=q_feat[b, h].rearrange("(p i) d -> p i d", i=TILES)
                 )
 
-        load_batch(0)
         wo_sb = const.tile([P, C_TILES, E], BF16)
         nc.sync.dma_start(out=wo_sb[:], in_=Wo.rearrange("(k p) e -> p k e", p=P))
+        load_batch(0)
         load_batch(1)
         bias = const.tile([P, C], BF16)
         nc.sync.dma_start(out=bias[:], in_=bo.partition_broadcast(P))
@@ -111,27 +111,25 @@ def tile_lineartransformerblock_pc_t_kernel(tc, q_feat, vk, k_sum, Wo, bo, out):
             rden[b] = per_batch.tile([P, TILES, H], F32, name="rden", tag="rden")
             nc.vector.reciprocal(out=rden[b][:], in_=den_sb[:])
 
-        def read_out(n):
+        def read_out(n, j):
             b, r = divmod(n, PAIRS)
-            a_sb[n] = per_pair.tile([P, PAIR, H, D], BF16, name="a_sb", tag="a_sb")
-            for j in range(PAIR):
-                i = r * PAIR + j
-                hs_ps = psum.tile([P, H, D], F32, tag="hs_ps", bufs=2)
-                for h in range(H):
-                    nc.tensor.matmul(
-                        hs_ps[:, h, :], lhsT=qT[b][:, h, i, :], rhs=vkT[b][:, h, :], start=True, stop=True
-                    )
-                nc.vector.tensor_tensor(
-                    out=a_sb[n][:, j, :, :],
-                    in0=hs_ps[:],
-                    in1=rden[b][:, i, :].unsqueeze(2).to_broadcast([P, H, D]),
-                    op=MULT,
+            i = r * PAIR + j
+            if j == 0:
+                a_sb[n] = per_pair.tile([P, PAIR, H, D], BF16, name="a_sb", tag="a_sb")
+            hs_ps = psum.tile([P, H, D], F32, tag="hs_ps", bufs=2)
+            for h in range(H):
+                nc.tensor.matmul(
+                    hs_ps[:, h, :], lhsT=qT[b][:, h, i, :], rhs=vkT[b][:, h, :], start=True, stop=True
+                )
+            for h in range(H):
+                nc.scalar.activation(
+                    out=a_sb[n][:, j, h, :], in_=hs_ps[:, h, :], func=COPY, scale=rden[b][:, i, h : h + 1]
                 )
 
         def flip_a(n):
             bank = transpose_blocks([a_sb[n][:, j, t, :] for j in range(PAIR) for t in range(PACK)])
             grouped[n] = per_pair.tile([P, PAIR, P, PACK], BF16, name="grouped", tag="grouped", align_bytes=64)
-            nc.scalar.copy(out=grouped[n][:], in_=bank[:].rearrange("p (j t) s -> p j s t", t=PACK))
+            nc.vector.tensor_copy(out=grouped[n][:], in_=bank[:].rearrange("p (j t) s -> p j s t", t=PACK))
 
         def quantise(n):
             codes[n] = per_pair.tile([P, PAIR * P], U32, name="codes", tag="codes", align_bytes=64)
@@ -169,11 +167,6 @@ def tile_lineartransformerblock_pc_t_kernel(tc, q_feat, vk, k_sum, Wo, bo, out):
         ksT = const.tile([P, B * H], BF16)
         nc.scalar.copy(out=ksT[:], in_=bank[:, 0, 0 : B * H])
 
-        flip_vk(0)
-        for h in range(H):
-            flip_q(0, h)
-        denominators(0)
-
         bank = transpose_blocks(
             [wo_sb[:, k, t * P : (t + 1) * P] for t in range(PACK) for k in range(C_TILES)]
         )
@@ -185,13 +178,14 @@ def tile_lineartransformerblock_pc_t_kernel(tc, q_feat, vk, k_sum, Wo, bo, out):
             out=wo_codes[:].bitcast(FP8X4), scales=wo_scales[:], in_=wo_grouped[:].rearrange("p c t -> p (c t)")
         )
 
-        for n in range(STEPS + 3):
+        flip_vk(0)
+        for h in range(H):
+            flip_q(0, h)
+        denominators(0)
+
+        for n in range(STEPS + 2):
             b, r = divmod(n, PAIRS)
             next_batch = n < STEPS and b + 1 < B
-            if n >= 3:
-                finish(n - 3)
-            if 2 <= n < STEPS + 2:
-                quantise(n - 2)
             if next_batch and r == 0:
                 flip_vk(b + 1)
             if next_batch:
@@ -199,8 +193,13 @@ def tile_lineartransformerblock_pc_t_kernel(tc, q_feat, vk, k_sum, Wo, bo, out):
             if 1 <= n < STEPS + 1:
                 flip_a(n - 1)
             if n < STEPS:
-                read_out(n)
-            if 2 <= n < STEPS + 2:
+                read_out(n, 0)
+            if n >= 2:
                 project(n - 2)
+                finish(n - 2)
+            if n < STEPS:
+                read_out(n, 1)
+            if 1 <= n < STEPS + 1:
+                quantise(n - 1)
             if next_batch and r == PAIRS - 1:
                 denominators(b + 1)

@@ -8,6 +8,7 @@ F32 = mybir.dt.float32
 U32 = mybir.dt.uint32
 U8 = mybir.dt.uint8
 FP8X4 = mybir.dt.float8_e4m3fn_x4
+MULT = mybir.AluOpType.mult
 ADD = mybir.AluOpType.add
 COPY = mybir.ActivationFunctionType.Copy
 
@@ -17,15 +18,15 @@ EPS = 1e-15
 
 P = 128
 PACK = 4
+HALVES = 2
 TILES = S // P
 PAIR = 2
 PAIRS = TILES // PAIR
 STEPS = B * PAIRS
-BANK_BLOCKS = 8
+HEADS = B * H
 C_TILES = C // P
 
 assert E == P * PACK
-assert H == PACK
 assert H == PAIRS
 
 FLOPS = 2 * B * S * E * C + 2 * B * H * S * D * D + 2 * B * H * S * D
@@ -36,17 +37,22 @@ def tile_lineartransformerblock_pc_t_kernel(tc, q_feat, vk, k_sum, Wo, bo, out):
     with ExitStack() as ctx:
         const = ctx.enter_context(tc.tile_pool(name="const", bufs=1))
         loads = ctx.enter_context(tc.tile_pool(name="loads", bufs=1))
-        per_batch = ctx.enter_context(tc.tile_pool(name="per_batch", bufs=2))
+        per_batch = ctx.enter_context(tc.tile_pool(name="per_batch", bufs=3))
         per_pair = ctx.enter_context(tc.tile_pool(name="per_pair", bufs=3))
         psum = ctx.enter_context(tc.psum_pool(name="psum", bufs=1))
         ctx.enter_context(tc.manual_schedule())
 
         ident = const.tile([P, P], BF16)
         masks.make_identity(nc, ident[:])
+        ident_words = const.tile([P, P], F32)
+        masks.make_identity(nc, ident_words[:])
 
         ks_rows = const.tile([P, D], BF16)
         nc.vector.memset(ks_rows[:], 0.0)
-        nc.sync.dma_start(out=ks_rows[0 : B * H, :], in_=k_sum.rearrange("b h d -> (b h) d"))
+        nc.sync.dma_start(out=ks_rows[0:HEADS, :], in_=k_sum.rearrange("b h d -> (b h) d"))
+
+        wo_sb = const.tile([P, C_TILES, E], BF16)
+        nc.sync.dma_start(out=wo_sb[:], in_=Wo.rearrange("(k p) e -> p k e", p=P))
 
         vk_sb = {}
         q_sb = {}
@@ -55,13 +61,11 @@ def tile_lineartransformerblock_pc_t_kernel(tc, q_feat, vk, k_sum, Wo, bo, out):
             vk_sb[b] = loads.tile([P, H, D], BF16, name="vk_sb%d" % b)
             nc.sync.dma_start(out=vk_sb[b][:], in_=vk[b].rearrange("h n d -> n h d"))
             for h in range(H):
-                q_sb[(b, h)] = loads.tile([P, TILES, D], BF16, name="q_sb%d_%d" % (b, h))
+                q_sb[b * H + h] = loads.tile([P, TILES, D], BF16, name="q_sb%d" % (b * H + h))
                 nc.sync.dma_start(
-                    out=q_sb[(b, h)][:], in_=q_feat[b, h].rearrange("(p i) d -> p i d", i=TILES)
+                    out=q_sb[b * H + h][:], in_=q_feat[b, h].rearrange("(p i) d -> p i d", i=TILES)
                 )
 
-        wo_sb = const.tile([P, C_TILES, E], BF16)
-        nc.sync.dma_start(out=wo_sb[:], in_=Wo.rearrange("(k p) e -> p k e", p=P))
         load_batch(0)
         load_batch(1)
         bias = const.tile([P, C], BF16)
@@ -71,6 +75,7 @@ def tile_lineartransformerblock_pc_t_kernel(tc, q_feat, vk, k_sum, Wo, bo, out):
 
         vkT = {}
         qT = {}
+        den_ps = {}
         rden = {}
         a_sb = {}
         grouped = {}
@@ -78,58 +83,73 @@ def tile_lineartransformerblock_pc_t_kernel(tc, q_feat, vk, k_sum, Wo, bo, out):
         scales = {}
         o_ps = {}
 
-        def transpose_blocks(blocks):
-            bank = psum.tile([P, BANK_BLOCKS, P], BF16, tag="flipped", bufs=4)
-            for j, block in enumerate(blocks):
-                nc.tensor.transpose(bank[:, j, :], block, ident[:])
-            return bank
-
         def flip_vk(b):
-            bank = transpose_blocks([vk_sb[b][:, h, :] for h in range(H)])
+            bank = psum.tile([P, TILES, P], BF16, tag="qT_ps", bufs=2)
+            for h in range(H):
+                nc.tensor.transpose(bank[:, h, :], vk_sb[b][:, h, :], ident[:])
             vkT[b] = per_batch.tile([P, H, D], BF16, name="vkT", tag="vkT")
             nc.scalar.copy(out=vkT[b][:], in_=bank[:, 0:H, :])
 
-        def flip_q(b, h):
+        def flip_q(unit):
+            b, h = divmod(unit, H)
             if h == 0:
                 qT[b] = per_batch.tile([P, H, TILES, P], BF16, name="qT", tag="qT")
-            bank = transpose_blocks([q_sb[(b, h)][:, i, :] for i in range(TILES)])
+            bank = psum.tile([P, TILES, P], BF16, tag="qT_ps", bufs=2)
+            for i in range(TILES):
+                nc.tensor.transpose(bank[:, i, :], q_sb[unit][:, i, :], ident[:])
             nc.scalar.copy(out=qT[b][:, h, :, :], in_=bank[:])
 
-        def denominators(b):
-            den_ps = psum.tile([P, TILES, H], F32, tag="den_ps")
+        def denominators(unit):
+            b, h = divmod(unit, H)
+            if h == 0:
+                den_ps[b] = psum.tile([P, TILES, H], F32, name="den_ps", tag="den_ps")
             for i in range(TILES):
+                nc.tensor.matmul(
+                    den_ps[b][:, i, h : h + 1],
+                    lhsT=qT[b][:, h, i, :],
+                    rhs=ksT[:, unit : unit + 1],
+                    start=True,
+                    stop=True,
+                )
+            if h == H - 1:
+                den_sb = per_batch.tile([P, TILES, H], F32, tag="den_sb")
+                nc.vector.tensor_scalar_add(out=den_sb[:], in0=den_ps[b][:], scalar1=EPS)
+                rden[b] = per_batch.tile([P, TILES, H], F32, name="rden", tag="rden")
+                nc.vector.reciprocal(out=rden[b][:], in_=den_sb[:])
+
+        def read_out(n):
+            b, r = divmod(n, PAIRS)
+            a_sb[n] = per_pair.tile([P, PAIR, E], BF16, name="a_sb", tag="a_sb")
+            hs_ps = {}
+            for j in range(PAIR):
+                i = r * PAIR + j
+                hs_ps[j] = psum.tile([P, H, D], F32, name="hs_ps", tag="hs_ps", bufs=2)
                 for h in range(H):
                     nc.tensor.matmul(
-                        den_ps[:, i, h : h + 1],
-                        lhsT=qT[b][:, h, i, :],
-                        rhs=ksT[:, b * H + h : b * H + h + 1],
-                        start=True,
-                        stop=True,
+                        hs_ps[j][:, h, :], lhsT=qT[b][:, h, i, :], rhs=vkT[b][:, h, :], start=True, stop=True
                     )
-            den_sb = per_batch.tile([P, TILES, H], F32, tag="den_sb")
-            nc.vector.tensor_scalar_add(out=den_sb[:], in0=den_ps[:], scalar1=EPS)
-            rden[b] = per_batch.tile([P, TILES, H], F32, name="rden", tag="rden")
-            nc.vector.reciprocal(out=rden[b][:], in_=den_sb[:])
-
-        def read_out(n, j):
-            b, r = divmod(n, PAIRS)
-            i = r * PAIR + j
-            if j == 0:
-                a_sb[n] = per_pair.tile([P, PAIR, H, D], BF16, name="a_sb", tag="a_sb")
-            hs_ps = psum.tile([P, H, D], F32, tag="hs_ps", bufs=2)
-            for h in range(H):
-                nc.tensor.matmul(
-                    hs_ps[:, h, :], lhsT=qT[b][:, h, i, :], rhs=vkT[b][:, h, :], start=True, stop=True
-                )
+            nc.vector.tensor_tensor(
+                out=a_sb[n][:, 0, :].rearrange("p (h n) -> p h n", h=H),
+                in0=hs_ps[0][:],
+                in1=rden[b][:, r * PAIR, :].unsqueeze(2).to_broadcast([P, H, D]),
+                op=MULT,
+            )
             for h in range(H):
                 nc.scalar.activation(
-                    out=a_sb[n][:, j, h, :], in_=hs_ps[:, h, :], func=COPY, scale=rden[b][:, i, h : h + 1]
+                    out=a_sb[n][:, 1, h * D : (h + 1) * D],
+                    in_=hs_ps[1][:, h, :],
+                    func=COPY,
+                    scale=rden[b][:, r * PAIR + 1, h : h + 1],
                 )
 
         def flip_a(n):
-            bank = transpose_blocks([a_sb[n][:, j, t, :] for j in range(PAIR) for t in range(PACK)])
+            bank = psum.tile([P, PAIR, HALVES, P], F32, tag="aT_ps", bufs=2)
+            for j in range(PAIR):
+                words = a_sb[n][:, j, :].bitcast(F32)
+                for u in range(HALVES):
+                    nc.tensor.transpose(bank[:, j, u, :], words[:, u * P : (u + 1) * P], ident_words[:])
             grouped[n] = per_pair.tile([P, PAIR, P, PACK], BF16, name="grouped", tag="grouped", align_bytes=64)
-            nc.vector.tensor_copy(out=grouped[n][:], in_=bank[:].rearrange("p (j t) s -> p j s t", t=PACK))
+            nc.scalar.copy(out=grouped[n][:].bitcast(F32), in_=bank[:].rearrange("p j u s -> p j s u"))
 
         def quantise(n):
             codes[n] = per_pair.tile([P, PAIR * P], U32, name="codes", tag="codes", align_bytes=64)
@@ -163,15 +183,20 @@ def tile_lineartransformerblock_pc_t_kernel(tc, q_feat, vk, k_sum, Wo, bo, out):
             rows = out[b].rearrange("(p i) c -> p i c", i=TILES)
             nc.sync.dma_start(out=rows[:, r * PAIR : (r + 1) * PAIR, :], in_=o_sb[:])
 
-        bank = transpose_blocks([ks_rows[:]])
-        ksT = const.tile([P, B * H], BF16)
-        nc.scalar.copy(out=ksT[:], in_=bank[:, 0, 0 : B * H])
+        bank = psum.tile([P, TILES, P], BF16, tag="qT_ps", bufs=2)
+        nc.tensor.transpose(bank[:, 0, :], ks_rows[:], ident[:])
+        ksT = const.tile([P, HEADS], BF16)
+        nc.scalar.copy(out=ksT[:], in_=bank[:, 0, 0:HEADS])
 
-        bank = transpose_blocks(
-            [wo_sb[:, k, t * P : (t + 1) * P] for t in range(PACK) for k in range(C_TILES)]
-        )
+        wo_bank = psum.tile([P, HALVES, C], F32, tag="aT_ps", bufs=2)
+        for k in range(C_TILES):
+            words = wo_sb[:, k, :].bitcast(F32)
+            for u in range(HALVES):
+                nc.tensor.transpose(
+                    wo_bank[:, u, k * P : (k + 1) * P], words[:, u * P : (u + 1) * P], ident_words[:]
+                )
         wo_grouped = const.tile([P, C, PACK], BF16, align_bytes=64)
-        nc.scalar.copy(out=wo_grouped[:], in_=bank[:].rearrange("p (t k) c -> p (k c) t", t=PACK))
+        nc.scalar.copy(out=wo_grouped[:].bitcast(F32), in_=wo_bank[:].rearrange("p u c -> p c u"))
         wo_codes = const.tile([P, C], U32, align_bytes=64)
         wo_scales = const.tile([P, C], U8, align_bytes=64)
         nc.vector.quantize_mx(
@@ -179,27 +204,25 @@ def tile_lineartransformerblock_pc_t_kernel(tc, q_feat, vk, k_sum, Wo, bo, out):
         )
 
         flip_vk(0)
-        for h in range(H):
-            flip_q(0, h)
-        denominators(0)
+        for unit in range(H + 1):
+            flip_q(unit)
+        for unit in range(H):
+            denominators(unit)
 
         for n in range(STEPS + 2):
             b, r = divmod(n, PAIRS)
-            next_batch = n < STEPS and b + 1 < B
-            if next_batch and r == 0:
+            if n < STEPS:
+                read_out(n)
+            if n + H + 1 < HEADS:
+                flip_q(n + H + 1)
+            if r == 0 and b + 1 < B:
                 flip_vk(b + 1)
-            if next_batch:
-                flip_q(b + 1, r)
             if 1 <= n < STEPS + 1:
                 flip_a(n - 1)
-            if n < STEPS:
-                read_out(n, 0)
             if n >= 2:
                 project(n - 2)
                 finish(n - 2)
-            if n < STEPS:
-                read_out(n, 1)
             if 1 <= n < STEPS + 1:
                 quantise(n - 1)
-            if next_batch and r == PAIRS - 1:
-                denominators(b + 1)
+            if n + H < HEADS:
+                denominators(n + H)

@@ -10,7 +10,6 @@ U8 = mybir.dt.uint8
 FP8X4 = mybir.dt.float8_e4m3fn_x4
 MULT = mybir.AluOpType.mult
 ADD = mybir.AluOpType.add
-COPY = mybir.ActivationFunctionType.Copy
 
 B, H, S, D, C = 8, 4, 1024, 128, 256
 E = H * D
@@ -68,8 +67,10 @@ def tile_lineartransformerblock_pc_t_kernel(tc, q_feat, vk, k_sum, Wo, bo, out):
 
         load_batch(0)
         load_batch(1)
-        bias = const.tile([P, C], BF16)
-        nc.sync.dma_start(out=bias[:], in_=bo.partition_broadcast(P))
+        bo_rows = const.tile([P, C], BF16)
+        nc.sync.dma_start(out=bo_rows[:], in_=bo.partition_broadcast(P))
+        bias = const.tile([P, C], F32)
+        nc.gpsimd.tensor_copy(out=bias[:], in_=bo_rows[:])
         for b in range(2, B):
             load_batch(b)
 
@@ -120,30 +121,22 @@ def tile_lineartransformerblock_pc_t_kernel(tc, q_feat, vk, k_sum, Wo, bo, out):
         def read_out(n):
             b, r = divmod(n, PAIRS)
             a_sb[n] = per_pair.tile([P, PAIR, E], BF16, name="a_sb", tag="a_sb")
-            hs_ps = {}
             for j in range(PAIR):
                 i = r * PAIR + j
-                hs_ps[j] = psum.tile([P, H, D], F32, name="hs_ps", tag="hs_ps", bufs=2)
+                hs_ps = psum.tile([P, H, D], F32, tag="hs_ps", bufs=2)
                 for h in range(H):
                     nc.tensor.matmul(
-                        hs_ps[j][:, h, :], lhsT=qT[b][:, h, i, :], rhs=vkT[b][:, h, :], start=True, stop=True
+                        hs_ps[:, h, :], lhsT=qT[b][:, h, i, :], rhs=vkT[b][:, h, :], start=True, stop=True
                     )
-            nc.vector.tensor_tensor(
-                out=a_sb[n][:, 0, :].rearrange("p (h n) -> p h n", h=H),
-                in0=hs_ps[0][:],
-                in1=rden[b][:, r * PAIR, :].unsqueeze(2).to_broadcast([P, H, D]),
-                op=MULT,
-            )
-            for h in range(H):
-                nc.scalar.activation(
-                    out=a_sb[n][:, 1, h * D : (h + 1) * D],
-                    in_=hs_ps[1][:, h, :],
-                    func=COPY,
-                    scale=rden[b][:, r * PAIR + 1, h : h + 1],
+                nc.vector.tensor_tensor(
+                    out=a_sb[n][:, j, :].rearrange("p (h n) -> p h n", h=H),
+                    in0=hs_ps[:],
+                    in1=rden[b][:, i, :].unsqueeze(2).to_broadcast([P, H, D]),
+                    op=MULT,
                 )
 
         def flip_a(n):
-            bank = psum.tile([P, PAIR, HALVES, P], F32, tag="aT_ps", bufs=2)
+            bank = psum.tile([P, PAIR, HALVES, P], F32, tag="aT_ps")
             for j in range(PAIR):
                 words = a_sb[n][:, j, :].bitcast(F32)
                 for u in range(HALVES):
@@ -161,7 +154,7 @@ def tile_lineartransformerblock_pc_t_kernel(tc, q_feat, vk, k_sum, Wo, bo, out):
             )
 
         def project(n):
-            o_ps[n] = psum.tile([P, PAIR, C], F32, name="o_ps", tag="o_ps")
+            o_ps[n] = psum.tile([P, PAIR, C], F32, name="o_ps", tag="o_ps", bufs=2)
             for j in range(PAIR):
                 tokens = slice(j * P, (j + 1) * P)
                 nc.tensor.matmul_mx(
@@ -177,8 +170,9 @@ def tile_lineartransformerblock_pc_t_kernel(tc, q_feat, vk, k_sum, Wo, bo, out):
         def finish(n):
             b, r = divmod(n, PAIRS)
             o_sb = per_pair.tile([P, PAIR, C], F32, tag="o_sb", bufs=4)
-            nc.vector.tensor_tensor(
-                out=o_sb[:], in0=o_ps[n][:], in1=bias[:].unsqueeze(1).to_broadcast([P, PAIR, C]), op=ADD
+            nc.scalar.copy(out=o_sb[:], in_=o_ps[n][:])
+            nc.gpsimd.tensor_tensor(
+                out=o_sb[:], in0=o_sb[:], in1=bias[:].unsqueeze(1).to_broadcast([P, PAIR, C]), op=ADD
             )
             rows = out[b].rearrange("(p i) c -> p i c", i=TILES)
             nc.sync.dma_start(out=rows[:, r * PAIR : (r + 1) * PAIR, :], in_=o_sb[:])
@@ -188,7 +182,7 @@ def tile_lineartransformerblock_pc_t_kernel(tc, q_feat, vk, k_sum, Wo, bo, out):
         ksT = const.tile([P, HEADS], BF16)
         nc.scalar.copy(out=ksT[:], in_=bank[:, 0, 0:HEADS])
 
-        wo_bank = psum.tile([P, HALVES, C], F32, tag="aT_ps", bufs=2)
+        wo_bank = psum.tile([P, HALVES, C], F32, tag="aT_ps")
         for k in range(C_TILES):
             words = wo_sb[:, k, :].bitcast(F32)
             for u in range(HALVES):
@@ -211,6 +205,8 @@ def tile_lineartransformerblock_pc_t_kernel(tc, q_feat, vk, k_sum, Wo, bo, out):
 
         for n in range(STEPS + 2):
             b, r = divmod(n, PAIRS)
+            if n >= 2:
+                quantise(n - 2)
             if n < STEPS:
                 read_out(n)
             if n + H + 1 < HEADS:
@@ -222,7 +218,5 @@ def tile_lineartransformerblock_pc_t_kernel(tc, q_feat, vk, k_sum, Wo, bo, out):
             if n >= 2:
                 project(n - 2)
                 finish(n - 2)
-            if 1 <= n < STEPS + 1:
-                quantise(n - 1)
             if n + H < HEADS:
                 denominators(n + H)

@@ -89,7 +89,7 @@ def tile_lineartransformerblock_pc_t_kernel(tc, q_feat, vk, k_sum, Wo, bo, out):
             for h in range(H):
                 nc.tensor.transpose(bank[:, h, :], vk_sb[b][:, h, :], ident[:])
             vkT[b] = per_batch.tile([P, H, D], BF16, name="vkT", tag="vkT")
-            nc.scalar.copy(out=vkT[b][:], in_=bank[:, 0:H, :])
+            nc.scalar.copy(out=vkT[b][:].bitcast(F32), in_=bank[:, 0:H, :].bitcast(F32))
 
         def flip_q(unit):
             b, h = divmod(unit, H)
@@ -98,7 +98,7 @@ def tile_lineartransformerblock_pc_t_kernel(tc, q_feat, vk, k_sum, Wo, bo, out):
             bank = psum.tile([P, TILES, P], BF16, tag="qT_ps", bufs=2)
             for i in range(TILES):
                 nc.tensor.transpose(bank[:, i, :], q_sb[unit][:, i, :], ident[:])
-            nc.scalar.copy(out=qT[b][:, h, :, :], in_=bank[:])
+            nc.scalar.copy(out=qT[b][:, h, :, :].bitcast(F32), in_=bank[:].bitcast(F32))
 
         def denominators(unit):
             b, h = divmod(unit, H)

@@ -22,11 +22,9 @@ TILES = S // P
 PAIR = 2
 PAIRS = TILES // PAIR
 STEPS = B * PAIRS
-HEADS = B * H
 C_TILES = C // P
 
 assert E == P * PACK
-assert H == PAIRS
 
 FLOPS = 2 * B * S * E * C + 2 * B * H * S * D * D + 2 * B * H * S * D
 
@@ -36,8 +34,8 @@ def tile_lineartransformerblock_pc_t_kernel(tc, q_feat, vk, k_sum, Wo, bo, out):
     with ExitStack() as ctx:
         const = ctx.enter_context(tc.tile_pool(name="const", bufs=1))
         loads = ctx.enter_context(tc.tile_pool(name="loads", bufs=1))
-        per_batch = ctx.enter_context(tc.tile_pool(name="per_batch", bufs=3))
-        per_pair = ctx.enter_context(tc.tile_pool(name="per_pair", bufs=3))
+        per_batch = ctx.enter_context(tc.tile_pool(name="per_batch", bufs=2))
+        per_pair = ctx.enter_context(tc.tile_pool(name="per_pair", bufs=4))
         psum = ctx.enter_context(tc.psum_pool(name="psum", bufs=1))
         ctx.enter_context(tc.manual_schedule())
 
@@ -48,7 +46,7 @@ def tile_lineartransformerblock_pc_t_kernel(tc, q_feat, vk, k_sum, Wo, bo, out):
 
         ks_rows = const.tile([P, D], BF16)
         nc.vector.memset(ks_rows[:], 0.0)
-        nc.sync.dma_start(out=ks_rows[0:HEADS, :], in_=k_sum.rearrange("b h d -> (b h) d"))
+        nc.sync.dma_start(out=ks_rows[0 : B * H, :], in_=k_sum.rearrange("b h d -> (b h) d"))
 
         wo_sb = const.tile([P, C_TILES, E], BF16)
         nc.sync.dma_start(out=wo_sb[:], in_=Wo.rearrange("(k p) e -> p k e", p=P))
@@ -59,11 +57,11 @@ def tile_lineartransformerblock_pc_t_kernel(tc, q_feat, vk, k_sum, Wo, bo, out):
         def load_batch(b):
             vk_sb[b] = loads.tile([P, H, D], BF16, name="vk_sb%d" % b)
             nc.sync.dma_start(out=vk_sb[b][:], in_=vk[b].rearrange("h n d -> n h d"))
-            for h in range(H):
-                q_sb[b * H + h] = loads.tile([P, TILES, D], BF16, name="q_sb%d" % (b * H + h))
-                nc.sync.dma_start(
-                    out=q_sb[b * H + h][:], in_=q_feat[b, h].rearrange("(p i) d -> p i d", i=TILES)
-                )
+            tokens = q_feat[b].rearrange("h (p i) d -> p h i d", i=TILES)
+            for r in range(PAIRS):
+                n = b * PAIRS + r
+                q_sb[n] = loads.tile([P, H, PAIR, D], BF16, name="q_sb%d" % n)
+                nc.sync.dma_start(out=q_sb[n][:], in_=tokens[:, :, r * PAIR : (r + 1) * PAIR, :])
 
         load_batch(0)
         load_batch(1)
@@ -76,7 +74,6 @@ def tile_lineartransformerblock_pc_t_kernel(tc, q_feat, vk, k_sum, Wo, bo, out):
 
         vkT = {}
         qT = {}
-        den_ps = {}
         rden = {}
         a_sb = {}
         grouped = {}
@@ -85,53 +82,50 @@ def tile_lineartransformerblock_pc_t_kernel(tc, q_feat, vk, k_sum, Wo, bo, out):
         o_ps = {}
 
         def flip_vk(b):
-            bank = psum.tile([P, TILES, P], BF16, tag="qT_ps", bufs=2)
+            bank = psum.tile([P, H, PAIR, P], BF16, tag="qT_ps", bufs=2)
             for h in range(H):
-                nc.tensor.transpose(bank[:, h, :], vk_sb[b][:, h, :], ident[:])
+                nc.tensor.transpose(bank[:, h, 0, :], vk_sb[b][:, h, :], ident[:])
             vkT[b] = per_batch.tile([P, H, D], BF16, name="vkT", tag="vkT")
-            nc.scalar.copy(out=vkT[b][:].bitcast(F32), in_=bank[:, 0:H, :].bitcast(F32))
+            nc.scalar.copy(out=vkT[b][:], in_=bank[:, :, 0, :])
 
-        def flip_q(unit):
-            b, h = divmod(unit, H)
-            if h == 0:
-                qT[b] = per_batch.tile([P, H, TILES, P], BF16, name="qT", tag="qT")
-            bank = psum.tile([P, TILES, P], BF16, tag="qT_ps", bufs=2)
-            for i in range(TILES):
-                nc.tensor.transpose(bank[:, i, :], q_sb[unit][:, i, :], ident[:])
-            nc.scalar.copy(out=qT[b][:, h, :, :].bitcast(F32), in_=bank[:].bitcast(F32))
+        def flip_q(n):
+            bank = psum.tile([P, H, PAIR, P], BF16, tag="qT_ps", bufs=2)
+            for h in range(H):
+                for j in range(PAIR):
+                    nc.tensor.transpose(bank[:, h, j, :], q_sb[n][:, h, j, :], ident[:])
+            qT[n] = per_pair.tile([P, H, PAIR, P], BF16, name="qT", tag="qT")
+            nc.scalar.copy(out=qT[n][:], in_=bank[:])
 
-        def denominators(unit):
-            b, h = divmod(unit, H)
-            if h == 0:
-                den_ps[b] = psum.tile([P, TILES, H], F32, name="den_ps", tag="den_ps")
-            for i in range(TILES):
-                nc.tensor.matmul(
-                    den_ps[b][:, i, h : h + 1],
-                    lhsT=qT[b][:, h, i, :],
-                    rhs=ksT[:, unit : unit + 1],
-                    start=True,
-                    stop=True,
-                )
-            if h == H - 1:
-                den_sb = per_batch.tile([P, TILES, H], F32, tag="den_sb")
-                nc.vector.tensor_scalar_add(out=den_sb[:], in0=den_ps[b][:], scalar1=EPS)
-                rden[b] = per_batch.tile([P, TILES, H], F32, name="rden", tag="rden")
-                nc.vector.reciprocal(out=rden[b][:], in_=den_sb[:])
+        def denominators(n):
+            b = n // PAIRS
+            den_ps = psum.tile([P, PAIR, H], F32, tag="den_ps")
+            for j in range(PAIR):
+                for h in range(H):
+                    nc.tensor.matmul(
+                        den_ps[:, j, h : h + 1],
+                        lhsT=qT[n][:, h, j, :],
+                        rhs=ksT[:, b * H + h : b * H + h + 1],
+                        start=True,
+                        stop=True,
+                    )
+            den_sb = per_pair.tile([P, PAIR, H], F32, tag="den_sb")
+            nc.vector.tensor_scalar_add(out=den_sb[:], in0=den_ps[:], scalar1=EPS)
+            rden[n] = per_pair.tile([P, PAIR, H], F32, name="rden", tag="rden")
+            nc.vector.reciprocal(out=rden[n][:], in_=den_sb[:])
 
         def read_out(n):
-            b, r = divmod(n, PAIRS)
+            b = n // PAIRS
             a_sb[n] = per_pair.tile([P, PAIR, E], BF16, name="a_sb", tag="a_sb")
             for j in range(PAIR):
-                i = r * PAIR + j
                 hs_ps = psum.tile([P, H, D], F32, tag="hs_ps", bufs=2)
                 for h in range(H):
                     nc.tensor.matmul(
-                        hs_ps[:, h, :], lhsT=qT[b][:, h, i, :], rhs=vkT[b][:, h, :], start=True, stop=True
+                        hs_ps[:, h, :], lhsT=qT[n][:, h, j, :], rhs=vkT[b][:, h, :], start=True, stop=True
                     )
                 nc.vector.tensor_tensor(
                     out=a_sb[n][:, j, :].rearrange("p (h n) -> p h n", h=H),
                     in0=hs_ps[:],
-                    in1=rden[b][:, i, :].unsqueeze(2).to_broadcast([P, H, D]),
+                    in1=rden[n][:, j, :].unsqueeze(2).to_broadcast([P, H, D]),
                     op=MULT,
                 )
 
@@ -169,7 +163,7 @@ def tile_lineartransformerblock_pc_t_kernel(tc, q_feat, vk, k_sum, Wo, bo, out):
 
         def finish(n):
             b, r = divmod(n, PAIRS)
-            o_sb = per_pair.tile([P, PAIR, C], F32, tag="o_sb", bufs=4)
+            o_sb = per_pair.tile([P, PAIR, C], F32, tag="o_sb")
             nc.scalar.copy(out=o_sb[:], in_=o_ps[n][:])
             nc.gpsimd.tensor_tensor(
                 out=o_sb[:], in0=o_sb[:], in1=bias[:].unsqueeze(1).to_broadcast([P, PAIR, C]), op=ADD
@@ -177,10 +171,10 @@ def tile_lineartransformerblock_pc_t_kernel(tc, q_feat, vk, k_sum, Wo, bo, out):
             rows = out[b].rearrange("(p i) c -> p i c", i=TILES)
             nc.sync.dma_start(out=rows[:, r * PAIR : (r + 1) * PAIR, :], in_=o_sb[:])
 
-        bank = psum.tile([P, TILES, P], BF16, tag="qT_ps", bufs=2)
-        nc.tensor.transpose(bank[:, 0, :], ks_rows[:], ident[:])
-        ksT = const.tile([P, HEADS], BF16)
-        nc.scalar.copy(out=ksT[:], in_=bank[:, 0, 0:HEADS])
+        bank = psum.tile([P, H, PAIR, P], BF16, tag="qT_ps", bufs=2)
+        nc.tensor.transpose(bank[:, 0, 0, :], ks_rows[:], ident[:])
+        ksT = const.tile([P, B * H], BF16)
+        nc.scalar.copy(out=ksT[:], in_=bank[:, 0, 0, 0 : B * H])
 
         wo_bank = psum.tile([P, HALVES, C], F32, tag="aT_ps")
         for k in range(C_TILES):
@@ -198,25 +192,23 @@ def tile_lineartransformerblock_pc_t_kernel(tc, q_feat, vk, k_sum, Wo, bo, out):
         )
 
         flip_vk(0)
-        for unit in range(H + 1):
-            flip_q(unit)
-        for unit in range(H):
-            denominators(unit)
+        flip_q(0)
+        flip_q(1)
+        denominators(0)
 
         for n in range(STEPS + 2):
-            b, r = divmod(n, PAIRS)
             if n >= 2:
                 quantise(n - 2)
             if n < STEPS:
                 read_out(n)
-            if n + H + 1 < HEADS:
-                flip_q(n + H + 1)
-            if r == 0 and b + 1 < B:
-                flip_vk(b + 1)
             if 1 <= n < STEPS + 1:
                 flip_a(n - 1)
+            if n + 2 < STEPS:
+                flip_q(n + 2)
+            if (n + 2) % PAIRS == 0 and n + 2 < STEPS:
+                flip_vk((n + 2) // PAIRS)
+            if n + 1 < STEPS:
+                denominators(n + 1)
             if n >= 2:
                 project(n - 2)
                 finish(n - 2)
-            if n + H < HEADS:
-                denominators(n + H)

from contextlib import ExitStack

import concourse.masks as masks
import concourse.mybir as mybir

BF16 = mybir.dt.bfloat16
F32 = mybir.dt.float32
U32 = mybir.dt.uint32
U8 = mybir.dt.uint8
FP8X4 = mybir.dt.float8_e4m3fn_x4
MULT = mybir.AluOpType.mult
ADD = mybir.AluOpType.add

B, H, S, D, C = 8, 4, 1024, 128, 256
E = H * D
EPS = 1e-15

P = 128
PACK = 4
HALVES = 2
TILES = S // P
PAIR = 2
PAIRS = TILES // PAIR
STEPS = B * PAIRS
C_TILES = C // P

assert E == P * PACK

FLOPS = 2 * B * S * E * C + 2 * B * H * S * D * D + 2 * B * H * S * D


def tile_lineartransformerblock_pc_t_kernel(tc, q_feat, vk, k_sum, Wo, bo, out):
    nc = tc.nc
    with ExitStack() as ctx:
        const = ctx.enter_context(tc.tile_pool(name="const", bufs=1))
        loads = ctx.enter_context(tc.tile_pool(name="loads", bufs=1))
        per_batch = ctx.enter_context(tc.tile_pool(name="per_batch", bufs=2))
        per_pair = ctx.enter_context(tc.tile_pool(name="per_pair", bufs=4))
        psum = ctx.enter_context(tc.psum_pool(name="psum", bufs=1))
        ctx.enter_context(tc.manual_schedule())

        ident = const.tile([P, P], BF16)
        masks.make_identity(nc, ident[:])
        ident_words = const.tile([P, P], F32)
        masks.make_identity(nc, ident_words[:])

        ks_rows = const.tile([P, D], BF16)
        nc.vector.memset(ks_rows[:], 0.0)
        nc.sync.dma_start(out=ks_rows[0 : B * H, :], in_=k_sum.rearrange("b h d -> (b h) d"))

        wo_sb = const.tile([P, C_TILES, E], BF16)
        nc.sync.dma_start(out=wo_sb[:], in_=Wo.rearrange("(k p) e -> p k e", p=P))

        vk_sb = {}
        q_sb = {}

        def load_batch(b):
            vk_sb[b] = loads.tile([P, H, D], BF16, name="vk_sb%d" % b)
            nc.sync.dma_start(out=vk_sb[b][:], in_=vk[b].rearrange("h n d -> n h d"))
            tokens = q_feat[b].rearrange("h (p i) d -> p h i d", i=TILES)
            for r in range(PAIRS):
                n = b * PAIRS + r
                q_sb[n] = loads.tile([P, H, PAIR, D], BF16, name="q_sb%d" % n)
                nc.sync.dma_start(out=q_sb[n][:], in_=tokens[:, :, r * PAIR : (r + 1) * PAIR, :])

        load_batch(0)
        load_batch(1)
        bo_rows = const.tile([P, C], BF16)
        nc.sync.dma_start(out=bo_rows[:], in_=bo.partition_broadcast(P))
        bias = const.tile([P, C], F32)
        nc.gpsimd.tensor_copy(out=bias[:], in_=bo_rows[:])
        for b in range(2, B):
            load_batch(b)

        vkT = {}
        qT = {}
        rden = {}
        a_sb = {}
        grouped = {}
        codes = {}
        scales = {}
        o_ps = {}

        def flip_vk(b):
            bank = psum.tile([P, H, PAIR, P], BF16, tag="qT_ps", bufs=2)
            for h in range(H):
                nc.tensor.transpose(bank[:, h, 0, :], vk_sb[b][:, h, :], ident[:])
            vkT[b] = per_batch.tile([P, H, D], BF16, name="vkT", tag="vkT")
            nc.scalar.copy(out=vkT[b][:], in_=bank[:, :, 0, :])

        def flip_q(n):
            bank = psum.tile([P, H, PAIR, P], BF16, tag="qT_ps", bufs=2)
            for h in range(H):
                for j in range(PAIR):
                    nc.tensor.transpose(bank[:, h, j, :], q_sb[n][:, h, j, :], ident[:])
            qT[n] = per_pair.tile([P, H, PAIR, P], BF16, name="qT", tag="qT")
            nc.scalar.copy(out=qT[n][:], in_=bank[:])

        def denominators(n):
            b = n // PAIRS
            den_ps = psum.tile([P, PAIR, H], F32, tag="den_ps")
            for j in range(PAIR):
                for h in range(H):
                    nc.tensor.matmul(
                        den_ps[:, j, h : h + 1],
                        lhsT=qT[n][:, h, j, :],
                        rhs=ksT[:, b * H + h : b * H + h + 1],
                        start=True,
                        stop=True,
                    )
            den_sb = per_pair.tile([P, PAIR, H], F32, tag="den_sb")
            nc.vector.tensor_scalar_add(out=den_sb[:], in0=den_ps[:], scalar1=EPS)
            rden[n] = per_pair.tile([P, PAIR, H], F32, name="rden", tag="rden")
            nc.vector.reciprocal(out=rden[n][:], in_=den_sb[:])

        def read_out(n):
            b = n // PAIRS
            a_sb[n] = per_pair.tile([P, PAIR, E], BF16, name="a_sb", tag="a_sb")
            for j in range(PAIR):
                hs_ps = psum.tile([P, H, D], F32, tag="hs_ps", bufs=2)
                for h in range(H):
                    nc.tensor.matmul(
                        hs_ps[:, h, :], lhsT=qT[n][:, h, j, :], rhs=vkT[b][:, h, :], start=True, stop=True
                    )
                nc.vector.tensor_tensor(
                    out=a_sb[n][:, j, :].rearrange("p (h n) -> p h n", h=H),
                    in0=hs_ps[:],
                    in1=rden[n][:, j, :].unsqueeze(2).to_broadcast([P, H, D]),
                    op=MULT,
                )

        def flip_a(n):
            bank = psum.tile([P, PAIR, HALVES, P], F32, tag="aT_ps")
            for j in range(PAIR):
                words = a_sb[n][:, j, :].bitcast(F32)
                for u in range(HALVES):
                    nc.tensor.transpose(bank[:, j, u, :], words[:, u * P : (u + 1) * P], ident_words[:])
            grouped[n] = per_pair.tile([P, PAIR, P, PACK], BF16, name="grouped", tag="grouped", align_bytes=64)
            nc.scalar.copy(out=grouped[n][:].bitcast(F32), in_=bank[:].rearrange("p j u s -> p j s u"))

        def quantise(n):
            codes[n] = per_pair.tile([P, PAIR * P], U32, name="codes", tag="codes", align_bytes=64)
            scales[n] = per_pair.tile([P, PAIR * P], U8, name="scales", tag="scales", align_bytes=64)
            nc.vector.quantize_mx(
                out=codes[n][:].bitcast(FP8X4),
                scales=scales[n][:],
                in_=grouped[n][:].rearrange("p j s t -> p (j s t)"),
            )

        def project(n):
            o_ps[n] = psum.tile([P, PAIR, C], F32, name="o_ps", tag="o_ps", bufs=2)
            for j in range(PAIR):
                tokens = slice(j * P, (j + 1) * P)
                nc.tensor.matmul_mx(
                    out=o_ps[n][:, j, :],
                    lhsT=codes[n][:, tokens].bitcast(FP8X4),
                    lhsT_scale=scales[n][:, tokens],
                    rhs=wo_codes[:].bitcast(FP8X4),
                    rhs_scale=wo_scales[:],
                    start=True,
                    stop=True,
                )

        def finish(n):
            b, r = divmod(n, PAIRS)
            o_sb = per_pair.tile([P, PAIR, C], F32, tag="o_sb")
            nc.scalar.copy(out=o_sb[:], in_=o_ps[n][:])
            nc.gpsimd.tensor_tensor(
                out=o_sb[:], in0=o_sb[:], in1=bias[:].unsqueeze(1).to_broadcast([P, PAIR, C]), op=ADD
            )
            rows = out[b].rearrange("(p i) c -> p i c", i=TILES)
            nc.sync.dma_start(out=rows[:, r * PAIR : (r + 1) * PAIR, :], in_=o_sb[:])

        bank = psum.tile([P, H, PAIR, P], BF16, tag="qT_ps", bufs=2)
        nc.tensor.transpose(bank[:, 0, 0, :], ks_rows[:], ident[:])
        ksT = const.tile([P, B * H], BF16)
        nc.scalar.copy(out=ksT[:], in_=bank[:, 0, 0, 0 : B * H])

        wo_bank = psum.tile([P, HALVES, C], F32, tag="aT_ps")
        for k in range(C_TILES):
            words = wo_sb[:, k, :].bitcast(F32)
            for u in range(HALVES):
                nc.tensor.transpose(
                    wo_bank[:, u, k * P : (k + 1) * P], words[:, u * P : (u + 1) * P], ident_words[:]
                )
        wo_grouped = const.tile([P, C, PACK], BF16, align_bytes=64)
        nc.scalar.copy(out=wo_grouped[:].bitcast(F32), in_=wo_bank[:].rearrange("p u c -> p c u"))
        wo_codes = const.tile([P, C], U32, align_bytes=64)
        wo_scales = const.tile([P, C], U8, align_bytes=64)
        nc.vector.quantize_mx(
            out=wo_codes[:].bitcast(FP8X4), scales=wo_scales[:], in_=wo_grouped[:].rearrange("p c t -> p (c t)")
        )

        flip_vk(0)
        flip_q(0)
        flip_q(1)
        denominators(0)

        for n in range(STEPS + 2):
            if n >= 2:
                quantise(n - 2)
            if n < STEPS:
                read_out(n)
            if 1 <= n < STEPS + 1:
                flip_a(n - 1)
            if n + 2 < STEPS:
                flip_q(n + 2)
            if (n + 2) % PAIRS == 0 and n + 2 < STEPS:
                flip_vk((n + 2) // PAIRS)
            if n + 1 < STEPS:
                denominators(n + 1)
            if n >= 2:
                project(n - 2)
                finish(n - 2)
